import numpy as np
import ml_dtypes

BF16 = ml_dtypes.bfloat16


def bf(x):
    return np.asarray(x, np.float32).astype(BF16)


def f32(x):
    return np.asarray(x, np.float32)


def f64(x):
    return np.asarray(x).astype(np.float64)


def striped(idx):
    return np.tile(idx.reshape(-1, 16).T, (8, 1))


C, S, B, L, N = 256, 1024, 4, 256, 1024
BASE = 10000.0


def sinusoidal(length, d):
    i = np.arange(d // 2, dtype=np.float32)
    pos = np.arange(length, dtype=np.float32)[:, None]
    div = pos / np.power(np.float32(BASE), np.float32(2.0) * i / np.float32(d))
    pe = np.stack((np.sin(f64(div)), np.cos(f64(div))), axis=2).reshape(length, -1)
    return pe[:, :d]


def setup_inputs():
    return {"emb": f32(np.random.standard_normal((C, S))), "pe": f32(np.tile(sinusoidal(L, C).T, (1, B))), "offs": striped(np.random.permutation(np.tile(np.arange(S), 2))[:N])}


def reference(emb, pe, offs):
    idx = offs[:16].T.reshape(-1)
    return f64(emb)[:, idx] + f64(pe)

@@ -1,0 +1,31 @@
+import concourse.mybir as mybir
+
+F32 = mybir.dt.float32
+U16 = mybir.dt.uint16
+ADD = mybir.AluOpType.add
+
+P = 128
+C = 256
+WORDS = 1024
+N = 1024
+BLOCKS = C // P
+
+
+def tile_positionalembeddings_kernel(tc, emb, pe, offs, out):
+    nc = tc.nc
+    with (
+        tc.tile_pool(name="held", bufs=1) as held,
+        tc.tile_pool(name="work", bufs=BLOCKS) as work,
+    ):
+        offsets = held.tile([P, N // 16], U16, name="offsets")
+        nc.sync.dma_start(offsets[:], offs)
+
+        for b in range(BLOCKS):
+            rows = slice(b * P, (b + 1) * P)
+            table = work.tile([P, WORDS], F32, name="table")
+            position = work.tile([P, N], F32, name="position")
+            summed = work.tile([P, N], F32, name="summed")
+            nc.sync.dma_start(table[:], emb[rows, :])
+            nc.sync.dma_start(position[:], pe[rows, :])
+            nc.vector.tensor_tensor(summed[:], table[:].indirect(offsets[:]), position[:], ADD)
+            nc.sync.dma_start(out[rows, :], summed[:])

@@ -9,23 +9,30 @@ C = 256
 WORDS = 1024
 N = 1024
 BLOCKS = C // P
+PIECE = 256
+PIECES = N // PIECE
+PIECE_COLS = PIECE // 16
 
 
 def tile_positionalembeddings_kernel(tc, emb, pe, offs, out):
     nc = tc.nc
     with (
         tc.tile_pool(name="held", bufs=1) as held,
-        tc.tile_pool(name="work", bufs=BLOCKS) as work,
+        tc.tile_pool(name="tables", bufs=BLOCKS) as tables,
+        tc.tile_pool(name="work", bufs=BLOCKS * PIECES) as work,
     ):
         offsets = held.tile([P, N // 16], U16, name="offsets")
         nc.sync.dma_start(offsets[:], offs)
 
         for b in range(BLOCKS):
             rows = slice(b * P, (b + 1) * P)
-            table = work.tile([P, WORDS], F32, name="table")
-            position = work.tile([P, N], F32, name="position")
-            summed = work.tile([P, N], F32, name="summed")
+            table = tables.tile([P, WORDS], F32, name="table")
             nc.sync.dma_start(table[:], emb[rows, :])
-            nc.sync.dma_start(position[:], pe[rows, :])
-            nc.vector.tensor_tensor(summed[:], table[:].indirect(offsets[:]), position[:], ADD)
-            nc.sync.dma_start(out[rows, :], summed[:])
+            for s in range(PIECES):
+                cols = slice(s * PIECE, (s + 1) * PIECE)
+                position = work.tile([P, PIECE], F32, name="position")
+                summed = work.tile([P, PIECE], F32, name="summed")
+                nc.sync.dma_start(position[:], pe[rows, cols])
+                looked_up = table[:].indirect(offsets[:, s * PIECE_COLS : (s + 1) * PIECE_COLS])
+                nc.vector.tensor_tensor(summed[:], looked_up, position[:], ADD)
+                nc.scalar.dma_start(out[rows, cols], summed[:])

@@ -27,12 +27,12 @@ def tile_positionalembeddings_kernel(tc, emb, pe, offs, out):
         for b in range(BLOCKS):
             rows = slice(b * P, (b + 1) * P)
             table = tables.tile([P, WORDS], F32, name="table")
-            nc.sync.dma_start(table[:], emb[rows, :])
+            nc.scalar.dma_start(table[:], emb[rows, :])
             for s in range(PIECES):
                 cols = slice(s * PIECE, (s + 1) * PIECE)
                 position = work.tile([P, PIECE], F32, name="position")
                 summed = work.tile([P, PIECE], F32, name="summed")
-                nc.sync.dma_start(position[:], pe[rows, cols])
+                nc.scalar.dma_start(position[:], pe[rows, cols])
                 looked_up = table[:].indirect(offsets[:, s * PIECE_COLS : (s + 1) * PIECE_COLS])
                 nc.vector.tensor_tensor(summed[:], looked_up, position[:], ADD)
-                nc.scalar.dma_start(out[rows, cols], summed[:])
+                nc.sync.dma_start(out[rows, cols], summed[:])

@@ -18,21 +18,27 @@ def tile_positionalembeddings_kernel(tc, emb, pe, offs, out):
     nc = tc.nc
     with (
         tc.tile_pool(name="held", bufs=1) as held,
-        tc.tile_pool(name="tables", bufs=BLOCKS) as tables,
         tc.tile_pool(name="work", bufs=BLOCKS * PIECES) as work,
     ):
         offsets = held.tile([P, N // 16], U16, name="offsets")
         nc.sync.dma_start(offsets[:], offs)
 
+        tables = []
+        positions = []
         for b in range(BLOCKS):
             rows = slice(b * P, (b + 1) * P)
-            table = tables.tile([P, WORDS], F32, name="table")
-            nc.scalar.dma_start(table[:], emb[rows, :])
+            table = held.tile([P, WORDS], F32, name=f"table{b}")
+            nc.sync.dma_start(table[:], emb[rows, :])
+            tables.append(table)
             for s in range(PIECES):
-                cols = slice(s * PIECE, (s + 1) * PIECE)
-                position = work.tile([P, PIECE], F32, name="position")
+                position = held.tile([P, PIECE], F32, name=f"position{b}_{s}")
+                nc.sync.dma_start(position[:], pe[rows, s * PIECE : (s + 1) * PIECE])
+                positions.append(position)
+
+        for b in range(BLOCKS):
+            rows = slice(b * P, (b + 1) * P)
+            for s in range(PIECES):
                 summed = work.tile([P, PIECE], F32, name="summed")
-                nc.scalar.dma_start(position[:], pe[rows, cols])
-                looked_up = table[:].indirect(offsets[:, s * PIECE_COLS : (s + 1) * PIECE_COLS])
-                nc.vector.tensor_tensor(summed[:], looked_up, position[:], ADD)
-                nc.sync.dma_start(out[rows, cols], summed[:])
+                looked_up = tables[b][:].indirect(offsets[:, s * PIECE_COLS : (s + 1) * PIECE_COLS])
+                nc.vector.tensor_tensor(summed[:], looked_up, positions[b * PIECES + s][:], ADD)
+                nc.sync.dma_start(out[rows, s * PIECE : (s + 1) * PIECE], summed[:])

@@ -9,36 +9,34 @@ C = 256
 WORDS = 1024
 N = 1024
 BLOCKS = C // P
-PIECE = 256
-PIECES = N // PIECE
-PIECE_COLS = PIECE // 16
+assert BLOCKS == 2
+
+RISING = (128, 128, 256, 512)
+FALLING = tuple(reversed(RISING))
+assert sum(RISING) == N
 
 
 def tile_positionalembeddings_kernel(tc, emb, pe, offs, out):
     nc = tc.nc
     with (
         tc.tile_pool(name="held", bufs=1) as held,
-        tc.tile_pool(name="work", bufs=BLOCKS * PIECES) as work,
+        tc.tile_pool(name="tables", bufs=BLOCKS) as tables,
+        tc.tile_pool(name="work", bufs=BLOCKS * len(RISING)) as work,
     ):
         offsets = held.tile([P, N // 16], U16, name="offsets")
         nc.sync.dma_start(offsets[:], offs)
 
-        tables = []
-        positions = []
-        for b in range(BLOCKS):
+        for b, widths in enumerate((RISING, FALLING)):
             rows = slice(b * P, (b + 1) * P)
-            table = held.tile([P, WORDS], F32, name=f"table{b}")
+            table = tables.tile([P, WORDS], F32, name="table")
             nc.sync.dma_start(table[:], emb[rows, :])
-            tables.append(table)
-            for s in range(PIECES):
-                position = held.tile([P, PIECE], F32, name=f"position{b}_{s}")
-                nc.sync.dma_start(position[:], pe[rows, s * PIECE : (s + 1) * PIECE])
-                positions.append(position)
-
-        for b in range(BLOCKS):
-            rows = slice(b * P, (b + 1) * P)
-            for s in range(PIECES):
-                summed = work.tile([P, PIECE], F32, name="summed")
-                looked_up = tables[b][:].indirect(offsets[:, s * PIECE_COLS : (s + 1) * PIECE_COLS])
-                nc.vector.tensor_tensor(summed[:], looked_up, positions[b * PIECES + s][:], ADD)
-                nc.sync.dma_start(out[rows, s * PIECE : (s + 1) * PIECE], summed[:])
+            first = 0
+            for width in widths:
+                cols = slice(first, first + width)
+                position = work.tile([P, width], F32, name="position")
+                summed = work.tile([P, width], F32, name="summed")
+                nc.sync.dma_start(position[:], pe[rows, cols])
+                looked_up = table[:].indirect(offsets[:, first // 16 : (first + width) // 16])
+                nc.vector.tensor_tensor(summed[:], looked_up, position[:], ADD)
+                nc.scalar.dma_start(out[rows, cols], summed[:])
+                first += width

@@ -24,12 +24,13 @@ def tile_positionalembeddings_kernel(tc, emb, pe, offs, out):
         tc.tile_pool(name="work", bufs=BLOCKS * len(RISING)) as work,
     ):
         offsets = held.tile([P, N // 16], U16, name="offsets")
-        nc.sync.dma_start(offsets[:], offs)
 
         for b, widths in enumerate((RISING, FALLING)):
             rows = slice(b * P, (b + 1) * P)
             table = tables.tile([P, WORDS], F32, name="table")
             nc.sync.dma_start(table[:], emb[rows, :])
+            if b == 0:
+                nc.sync.dma_start(offsets[:], offs)
             first = 0
             for width in widths:
                 cols = slice(first, first + width)

@@ -11,9 +11,15 @@ N = 1024
 BLOCKS = C // P
 assert BLOCKS == 2
 
-RISING = (128, 128, 256, 512)
-FALLING = tuple(reversed(RISING))
-assert sum(RISING) == N
+LOADS = ((128, 128, 256, 512), (512, 512))
+LOOKUPS = ((128, 128, 256, 512), (512, 256, 128, 128))
+STORES = ((256, 256, 512), (512, 256, 128, 128))
+
+
+def pieces(widths):
+    ends = [sum(widths[: k + 1]) for k in range(len(widths))]
+    assert ends[-1] == N
+    return [(end - width, end) for end, width in zip(ends, widths)]
 
 
 def tile_positionalembeddings_kernel(tc, emb, pe, offs, out):
@@ -21,23 +27,31 @@ def tile_positionalembeddings_kernel(tc, emb, pe, offs, out):
     with (
         tc.tile_pool(name="held", bufs=1) as held,
         tc.tile_pool(name="tables", bufs=BLOCKS) as tables,
-        tc.tile_pool(name="work", bufs=BLOCKS * len(RISING)) as work,
+        tc.tile_pool(name="work", bufs=8) as work,
     ):
         offsets = held.tile([P, N // 16], U16, name="offsets")
 
-        for b, widths in enumerate((RISING, FALLING)):
+        for b in range(BLOCKS):
             rows = slice(b * P, (b + 1) * P)
-            table = tables.tile([P, WORDS], F32, name="table")
+            table = tables.tile([P, WORDS], F32, name="table", align_bytes=256)
             nc.sync.dma_start(table[:], emb[rows, :])
             if b == 0:
                 nc.sync.dma_start(offsets[:], offs)
-            first = 0
-            for width in widths:
-                cols = slice(first, first + width)
-                position = work.tile([P, width], F32, name="position")
-                summed = work.tile([P, width], F32, name="summed")
-                nc.sync.dma_start(position[:], pe[rows, cols])
-                looked_up = table[:].indirect(offsets[:, first // 16 : (first + width) // 16])
-                nc.vector.tensor_tensor(summed[:], looked_up, position[:], ADD)
-                nc.scalar.dma_start(out[rows, cols], summed[:])
-                first += width
+            load_ends = dict(pieces(LOADS[b]))
+            store_ends = dict(pieces(STORES[b]))
+            for start, end in pieces(LOOKUPS[b]):
+                if start in load_ends:
+                    load_start, load_end = start, load_ends[start]
+                    position = work.tile([P, load_end - load_start], F32, name="position", align_bytes=256)
+                    nc.sync.dma_start(position[:], pe[rows, load_start:load_end])
+                if start in store_ends:
+                    store_start, store_end = start, store_ends[start]
+                    summed = work.tile([P, store_end - store_start], F32, name="summed", align_bytes=256)
+                nc.vector.tensor_tensor(
+                    summed[:, start - store_start : end - store_start],
+                    table[:].indirect(offsets[:, start // 16 : end // 16]),
+                    position[:, start - load_start : end - load_start],
+                    ADD,
+                )
+                if end == store_end:
+                    nc.scalar.dma_start(out[rows, store_start:store_end], summed[:])

@@ -11,9 +11,9 @@ N = 1024
 BLOCKS = C // P
 assert BLOCKS == 2
 
-LOADS = ((128, 128, 256, 512), (512, 512))
-LOOKUPS = ((128, 128, 256, 512), (512, 256, 128, 128))
-STORES = ((256, 256, 512), (512, 256, 128, 128))
+LOADS = ((128, 320, 576), (512, 512))
+LOOKUPS = ((128, 320, 576), (512, 384, 128))
+STORES = ((128, 320, 576), (512, 384, 128))
 
 
 def pieces(widths):

@@ -11,9 +11,9 @@ N = 1024
 BLOCKS = C // P
 assert BLOCKS == 2
 
-LOADS = ((128, 320, 576), (512, 512))
-LOOKUPS = ((128, 320, 576), (512, 384, 128))
-STORES = ((128, 320, 576), (512, 384, 128))
+LOADS = ((128, 320, 576), (256, 384, 384))
+LOOKUPS = ((128, 320, 576), (256, 384, 256, 128))
+STORES = ((128, 320, 576), (256, 384, 256, 128))
 
 
 def pieces(widths):

@@ -54,4 +54,6 @@ def tile_positionalembeddings_kernel(tc, emb, pe, offs, out):
                     ADD,
                 )
                 if end == store_end:
-                    nc.scalar.dma_start(out[rows, store_start:store_end], summed[:])
+                    is_last = b == BLOCKS - 1 and end == N
+                    store_queue = nc.sync if is_last else nc.scalar
+                    store_queue.dma_start(out[rows, store_start:store_end], summed[:])

import concourse.mybir as mybir

F32 = mybir.dt.float32
U16 = mybir.dt.uint16
ADD = mybir.AluOpType.add

P = 128
C = 256
WORDS = 1024
N = 1024
BLOCKS = C // P
assert BLOCKS == 2

LOADS = ((128, 320, 576), (256, 384, 384))
LOOKUPS = ((128, 320, 576), (256, 384, 256, 128))
STORES = ((128, 320, 576), (256, 384, 256, 128))


def pieces(widths):
    ends = [sum(widths[: k + 1]) for k in range(len(widths))]
    assert ends[-1] == N
    return [(end - width, end) for end, width in zip(ends, widths)]


def tile_positionalembeddings_kernel(tc, emb, pe, offs, out):
    nc = tc.nc
    with (
        tc.tile_pool(name="held", bufs=1) as held,
        tc.tile_pool(name="tables", bufs=BLOCKS) as tables,
        tc.tile_pool(name="work", bufs=8) as work,
    ):
        offsets = held.tile([P, N // 16], U16, name="offsets")

        for b in range(BLOCKS):
            rows = slice(b * P, (b + 1) * P)
            table = tables.tile([P, WORDS], F32, name="table", align_bytes=256)
            nc.sync.dma_start(table[:], emb[rows, :])
            if b == 0:
                nc.sync.dma_start(offsets[:], offs)
            load_ends = dict(pieces(LOADS[b]))
            store_ends = dict(pieces(STORES[b]))
            for start, end in pieces(LOOKUPS[b]):
                if start in load_ends:
                    load_start, load_end = start, load_ends[start]
                    position = work.tile([P, load_end - load_start], F32, name="position", align_bytes=256)
                    nc.sync.dma_start(position[:], pe[rows, load_start:load_end])
                if start in store_ends:
                    store_start, store_end = start, store_ends[start]
                    summed = work.tile([P, store_end - store_start], F32, name="summed", align_bytes=256)
                nc.vector.tensor_tensor(
                    summed[:, start - store_start : end - store_start],
                    table[:].indirect(offsets[:, start // 16 : end // 16]),
                    position[:, start - load_start : end - load_start],
                    ADD,
                )
                if end == store_end:
                    is_last = b == BLOCKS - 1 and end == N
                    store_queue = nc.sync if is_last else nc.scalar
                    store_queue.dma_start(out[rows, store_start:store_end], summed[:])
